import numpy as np
import ml_dtypes


def mxq(x, axis, fmt="e4m3"):
    dtype, down = {"e4m3": (ml_dtypes.float8_e4m3fn, 7), "e5m2": (ml_dtypes.float8_e5m2, 14)}[fmt]
    v = np.moveaxis(np.asarray(x, np.float32).astype(ml_dtypes.bfloat16).astype(np.float64), axis, -1)
    blocks = v.reshape(v.shape[:-1] + (-1, 32))
    amax = np.abs(blocks).max(-1, keepdims=True)
    byte = np.maximum(np.where(amax > 0, np.frexp(amax)[1] - 1 + 127, 0) - down, 1)
    scale = np.exp2(byte - 127.0)
    codes = (blocks / scale).astype(np.float32).astype(dtype).astype(np.float64)
    return np.moveaxis((codes * scale).reshape(v.shape), -1, axis)


WIDE = False


def mx_kscale(k):
    if not WIDE:
        return np.ones(k)
    levels = np.array([10, -10, 5, -5, 0])
    a = np.random.permutation(np.resize(levels, k // 512 * 4)).reshape(k // 512, 4)
    idx = np.arange(k)
    return np.exp2(a[idx // 512, idx % 128 // 32])


BF16 = ml_dtypes.bfloat16


def bf(x):
    return np.asarray(x, np.float32).astype(BF16)


def f64(x):
    return np.asarray(x).astype(np.float64)


B_, S, D_IN, D_OUT, N, RANK, ALPHA = 4, 128, 2048, 2048, 32, 16, 32
NR = N * RANK
SCALE = ALPHA / RANK


def setup_inputs():
    s, t = mx_kscale(D_IN), mx_kscale(NR)
    tn = t.reshape(N, RANK)
    return {"x": bf(np.random.standard_normal((B_, S, D_IN)) * s),
            "lora_A": bf(np.random.standard_normal((N, RANK, D_IN)) / np.sqrt(D_IN) / s * tn[:, :, None]),
            "lora_B": bf(np.random.standard_normal((N, D_OUT, RANK)) / np.sqrt(RANK) / tn[:, None, :]),
            "W": bf(np.random.standard_normal((D_OUT, D_IN)) / np.sqrt(D_IN) / s),
            "bias": bf(np.random.standard_normal(D_OUT) * 0.3),
            "lora_weights": bf((1.0 + 0.5 * np.random.standard_normal(N)) * 2.0 / N)}


def reference(x, lora_A, lora_B, W, bias, lora_weights):
    xq = mxq(f64(x), 2, "e4m3")
    h = xq @ mxq(f64(lora_A).reshape(NR, D_IN), 1, "e4m3").T
    coef = (SCALE * f64(lora_weights))[:, None, None]
    bc = (f64(lora_B) * coef).transpose(1, 0, 2).reshape(D_OUT, NR)
    lora_out = mxq(h, 2, "e4m3") @ mxq(bc, 1, "e4m3").T
    base = (xq @ mxq(f64(W), 1, "e4m3").T) + f64(bias)
    return base + lora_out

@@ -1,0 +1,239 @@
+from contextlib import ExitStack
+
+import concourse.mybir as mybir
+from concourse.masks import make_identity
+
+F32 = mybir.dt.float32
+BF16 = mybir.dt.bfloat16
+U32 = mybir.dt.uint32
+U8 = mybir.dt.uint8
+FP8X4 = mybir.dt.float8_e4m3fn_x4
+ADD = mybir.AluOpType.add
+MULT = mybir.AluOpType.mult
+COPY = mybir.ActivationFunctionType.Copy
+
+P = 128
+TOK = 512
+D = 2048
+O = 2048
+NR = 512
+SCALE = 2.0
+FLOPS = 2 * TOK * D * O + 2 * TOK * D * NR + 2 * TOK * NR * O
+
+
+def tile_replaced_compose_lora_pa_kernel(tc, x, lora_A, lora_B, W, bias, lora_weights, out):
+    nc = tc.nc
+    with ExitStack() as ctx:
+        const = ctx.enter_context(tc.tile_pool(name="const", bufs=1))
+        raw = ctx.enter_context(tc.tile_pool(name="raw", bufs=4))
+        bpool = ctx.enter_context(tc.tile_pool(name="bpool", bufs=2))
+        grp = ctx.enter_context(tc.tile_pool(name="grp", bufs=3))
+        outp = ctx.enter_context(tc.tile_pool(name="outp", bufs=6))
+        tps = ctx.enter_context(tc.psum_pool(name="tps", bufs=4))
+        accp = ctx.enter_context(tc.psum_pool(name="accp", bufs=4))
+        ctx.enter_context(tc.manual_schedule())
+
+        x_rows = x.rearrange("b s d -> (b s) d")
+        a_rows = lora_A.rearrange("n r d -> (n r) d").rearrange("(q t) d -> q (t d)", t=4)
+        b_rows = lora_B.rearrange("n (p l) r -> p n (l r)", l=16)
+        w_rows = W.rearrange("(a p) d -> p a d", p=P)
+        out_rows = out.rearrange("b s o -> (b s) o")
+
+        ident = const.tile([P, P], F32, name="ident")
+        make_identity(nc, ident[:])
+
+        xq = const.tile([P, 2048], U32, name="xq", align_bytes=64)
+        xs = const.tile([P, 2048], U8, name="xs", align_bytes=64)
+        aq = const.tile([P, 2048], U32, name="aq", align_bytes=64)
+        asc = const.tile([P, 2048], U8, name="asc", align_bytes=64)
+        wq = const.tile([P, 8192], U32, name="wq", align_bytes=64)
+        ws = const.tile([P, 8192], U8, name="ws", align_bytes=64)
+        bq = const.tile([P, 2048], U32, name="bq", align_bytes=64)
+        bs = const.tile([P, 2048], U8, name="bs", align_bytes=64)
+        hq = const.tile([P, 512], U32, name="hq", align_bytes=64)
+        hs = const.tile([P, 512], U8, name="hs", align_bytes=64)
+        hg = const.tile([P, 2048], BF16, name="hg", align_bytes=64)
+        bias_b = const.tile([P, O], BF16, name="bias_b")
+        lw_b = const.tile([P, 32], BF16, name="lw_b")
+        sel = const.tile([P, P], F32, name="sel")
+        coef1 = const.tile([P, 1], F32, name="coef1")
+        coef = const.tile([P, 1], F32, name="coef")
+
+        x_sb = raw.tile([P, 8192], BF16, tag="raw", name="x_sb")
+        for tt in range(4):
+            nc.sync.dma_start(out=x_sb[:, tt * D:(tt + 1) * D], in_=x_rows[tt * P:(tt + 1) * P, :])
+        a_sb = raw.tile([P, 8192], BF16, tag="raw", name="a_sb")
+        for half in range(2):
+            nc.sync.dma_start(out=a_sb[:, half * 4096:(half + 1) * 4096], in_=a_rows[:, half * 4096:(half + 1) * 4096])
+        nc.sync.dma_start(out=lw_b[:], in_=lora_weights.partition_broadcast(P))
+        b_sb = bpool.tile([P, 8192], BF16, tag="b", name="b_sb", align_bytes=64)
+        for half in range(2):
+            nc.sync.dma_start(
+                out=b_sb[:, half * 4096:(half + 1) * 4096].rearrange("p (n k) -> p n k", k=256),
+                in_=b_rows[:, half * 16:(half + 1) * 16, :],
+            )
+        nc.sync.dma_start(out=bias_b[:], in_=bias.partition_broadcast(P))
+
+        w_sb = []
+
+        def load_w(g):
+            w_t = raw.tile([P, 8192], BF16, tag="raw", name="w_sb%d" % g)
+            for half in range(2):
+                nc.sync.dma_start(
+                    out=w_t[:, half * 4096:(half + 1) * 4096].rearrange("p (a d) -> p a d", a=2),
+                    in_=w_rows[:, 4 * g + 2 * half:4 * g + 2 * half + 2, :],
+                )
+            w_sb.append(w_t)
+
+        load_w(0)
+        load_w(1)
+
+        def t_unit(words, first):
+            banks = []
+            for c in range(4):
+                bank = tps.tile([P, 512], F32, tag="tp", name="bank")
+                for u in range(2):
+                    for i in range(2):
+                        j = 2 * c + u
+                        col = (first + i) * 1024 + j * P
+                        nc.tensor.transpose(bank[:, (2 * u + i) * P:(2 * u + i + 1) * P], words[:, col:col + P], ident[:])
+                banks.append(bank)
+            return banks
+
+        def c_unit(banks, engines):
+            g_t = grp.tile([P, 4096], BF16, tag="grp", name="g_t", align_bytes=64)
+            g_w = g_t[:].bitcast(F32)
+            for c in range(4):
+                dst = g_w[:, c * 512:(c + 1) * 512].rearrange("p (k u) -> p k u", u=2)
+                src = banks[c][:].rearrange("p (u k) -> p k u", u=2)
+                if engines[c] == "s":
+                    nc.scalar.copy(out=dst, in_=src)
+                else:
+                    nc.vector.tensor_copy(out=dst, in_=src)
+            return g_t
+
+        for (src_t, codes, planes) in ((x_sb, xq, xs), (a_sb, aq, asc)):
+            words = src_t[:].bitcast(F32)
+            for pair in range(2):
+                banks = t_unit(words, 2 * pair)
+                g_t = c_unit(banks, "svsv")
+                nc.vector.quantize_mx(
+                    out=codes[:, pair * 1024:(pair + 1) * 1024].bitcast(FP8X4),
+                    scales=planes[:, pair * 1024:(pair + 1) * 1024],
+                    in_=g_t[:],
+                )
+        load_w(2)
+        load_w(3)
+
+        nc.vector.tensor_tensor(
+            out=sel[:].rearrange("p (n s) -> p n s", s=4),
+            in0=ident[:].rearrange("p (n s) -> p n s", s=4),
+            in1=lw_b[:].unsqueeze(2).to_broadcast([P, 32, 4]),
+            op=MULT,
+        )
+        nc.vector.tensor_reduce(out=coef1[:], in_=sel[:], axis=mybir.AxisListType.X, op=ADD)
+        nc.vector.tensor_scalar(out=coef[:], in0=coef1[:], scalar1=SCALE, scalar2=None, op0=MULT)
+
+        bl = bpool.tile([P, 8192], BF16, tag="b", name="bl", align_bytes=64)
+        b_w = b_sb[:].bitcast(F32).rearrange("p (n l s u) -> p l u n s", n=32, l=16, s=4, u=2)
+        bl_w = bl[:].bitcast(F32)
+        bl_v = bl_w.rearrange("p (l u n s) -> p l u n s", l=16, u=2, n=32, s=4)
+        for half in range(2):
+            for u in range(2):
+                nc.vector.tensor_copy(
+                    out=bl_v[:, :, u, half * 16:(half + 1) * 16, :],
+                    in_=b_w[:, :, u, half * 16:(half + 1) * 16, :],
+                )
+
+        for tt in range(4):
+            acc = accp.tile([P, 512], F32, tag="acc", name="acc")
+            x0 = (tt // 2) * 1024 + (tt % 2) * P
+            for t in range(4):
+                a0 = (t // 2) * 1024 + (t % 2) * P
+                for c in range(4):
+                    nc.tensor.matmul_mx(
+                        out=acc[:, t * P:(t + 1) * P],
+                        lhsT=aq[:, a0 + c * 256:a0 + c * 256 + P].bitcast(FP8X4),
+                        lhsT_scale=asc[:, a0 + c * 256:a0 + c * 256 + P],
+                        rhs=xq[:, x0 + c * 256:x0 + c * 256 + P].bitcast(FP8X4),
+                        rhs_scale=xs[:, x0 + c * 256:x0 + c * 256 + P],
+                        start=(c == 0),
+                        stop=(c == 3),
+                    )
+            nc.scalar.copy(
+                out=hg[:, tt * 512:(tt + 1) * 512].rearrange("q (r t) -> q r t", t=4),
+                in_=acc[:].rearrange("q (t r) -> q r t", t=4),
+            )
+        nc.vector.quantize_mx(out=hq[:].bitcast(FP8X4), scales=hs[:], in_=hg[:])
+
+        bg = bpool.tile([P, 8192], BF16, tag="b", name="bg", align_bytes=64)
+        bg_v = bg[:].rearrange("q (p l a e) -> q p l a e", p=P, l=8, a=4, e=2)
+        for lp in range(8):
+            bank = tps.tile([P, 512], F32, tag="tp", name="bankb")
+            for a in range(4):
+                col = (2 * lp + a // 2) * 256 + (a % 2) * P
+                nc.tensor.transpose(bank[:, a * P:(a + 1) * P], bl_w[:, col:col + P], ident[:])
+            src = bank[:].bitcast(BF16).rearrange("q (a p e) -> q p a e", a=4, e=2)
+            if (lp // 2) % 2 == 0:
+                nc.scalar.activation(out=bg_v[:, :, lp, :, :], in_=src, func=COPY, scale=coef[:, 0:1])
+            else:
+                nc.vector.tensor_scalar(out=bg_v[:, :, lp, :, :], in0=src, scalar1=coef[:, 0:1], scalar2=None, op0=MULT)
+        for half in range(2):
+            nc.vector.quantize_mx(
+                out=bq[:, half * 1024:(half + 1) * 1024].bitcast(FP8X4),
+                scales=bs[:, half * 1024:(half + 1) * 1024],
+                in_=bg[:, half * 4096:(half + 1) * 4096],
+            )
+
+        def w_t(g, pair):
+            return t_unit(w_sb[g][:].bitcast(F32), 2 * pair)
+
+        def w_cq(g, pair, banks):
+            g_t = c_unit(banks, "sssv")
+            for c in range(4):
+                o0 = g * 2048 + c * 512 + pair * 256
+                nc.vector.quantize_mx(
+                    out=wq[:, o0:o0 + 256].bitcast(FP8X4),
+                    scales=ws[:, o0:o0 + 256],
+                    in_=g_t[:, c * 1024:(c + 1) * 1024],
+                )
+
+        def mm(g, tt):
+            acc = accp.tile([P, 512], F32, tag="acc", name="acc")
+            x0 = (tt // 2) * 1024 + (tt % 2) * P
+            for c in range(4):
+                nc.tensor.matmul_mx(
+                    out=acc[:],
+                    lhsT=xq[:, x0 + c * 256:x0 + c * 256 + P].bitcast(FP8X4),
+                    lhsT_scale=xs[:, x0 + c * 256:x0 + c * 256 + P],
+                    rhs=wq[:, g * 2048 + c * 512:g * 2048 + (c + 1) * 512].bitcast(FP8X4),
+                    rhs_scale=ws[:, g * 2048 + c * 512:g * 2048 + (c + 1) * 512],
+                    start=(c == 0),
+                    stop=False,
+                )
+            nc.tensor.matmul_mx(
+                out=acc[:],
+                lhsT=hq[:, tt * P:(tt + 1) * P].bitcast(FP8X4),
+                lhsT_scale=hs[:, tt * P:(tt + 1) * P],
+                rhs=bq[:, g * 512:(g + 1) * 512].bitcast(FP8X4),
+                rhs_scale=bs[:, g * 512:(g + 1) * 512],
+                start=False,
+                stop=True,
+            )
+            return acc
+
+        def fin(g, tt, acc):
+            o_sb = outp.tile([P, 512], F32, tag="o", name="o_sb")
+            nc.vector.tensor_tensor(out=o_sb[:], in0=acc[:], in1=bias_b[:, g * 512:(g + 1) * 512], op=ADD)
+            nc.sync.dma_start(out=out_rows[tt * P:(tt + 1) * P, g * 512:(g + 1) * 512], in_=o_sb[:])
+
+        for pair in range(2):
+            w_cq(0, pair, w_t(0, pair))
+        for g in range(4):
+            for half in range(2):
+                accs = [mm(g, 2 * half), mm(g, 2 * half + 1)]
+                banks = w_t(g + 1, half) if g < 3 else None
+                fin(g, 2 * half, accs[0])
+                fin(g, 2 * half + 1, accs[1])
+                if g < 3:
+                    w_cq(g + 1, half, banks)

@@ -62,17 +62,10 @@ def tile_replaced_compose_lora_pa_kernel(tc, x, lora_A, lora_B, W, bias, lora_we
         x_sb = raw.tile([P, 8192], BF16, tag="raw", name="x_sb")
         for tt in range(4):
             nc.sync.dma_start(out=x_sb[:, tt * D:(tt + 1) * D], in_=x_rows[tt * P:(tt + 1) * P, :])
+        nc.sync.dma_start(out=lw_b[:], in_=lora_weights.partition_broadcast(P))
         a_sb = raw.tile([P, 8192], BF16, tag="raw", name="a_sb")
         for half in range(2):
             nc.sync.dma_start(out=a_sb[:, half * 4096:(half + 1) * 4096], in_=a_rows[:, half * 4096:(half + 1) * 4096])
-        nc.sync.dma_start(out=lw_b[:], in_=lora_weights.partition_broadcast(P))
-        b_sb = bpool.tile([P, 8192], BF16, tag="b", name="b_sb", align_bytes=64)
-        for half in range(2):
-            nc.sync.dma_start(
-                out=b_sb[:, half * 4096:(half + 1) * 4096].rearrange("p (n k) -> p n k", k=256),
-                in_=b_rows[:, half * 16:(half + 1) * 16, :],
-            )
-        nc.sync.dma_start(out=bias_b[:], in_=bias.partition_broadcast(P))
 
         w_sb = []
 
@@ -86,7 +79,14 @@ def tile_replaced_compose_lora_pa_kernel(tc, x, lora_A, lora_B, W, bias, lora_we
             w_sb.append(w_t)
 
         load_w(0)
+        b_sb = bpool.tile([P, 8192], BF16, tag="b", name="b_sb", align_bytes=64)
+        for half in range(2):
+            nc.sync.dma_start(
+                out=b_sb[:, half * 4096:(half + 1) * 4096].rearrange("p (n k) -> p n k", k=256),
+                in_=b_rows[:, half * 16:(half + 1) * 16, :],
+            )
         load_w(1)
+        nc.sync.dma_start(out=bias_b[:], in_=bias.partition_broadcast(P))
 
         def t_unit(words, first):
             banks = []
@@ -100,23 +100,20 @@ def tile_replaced_compose_lora_pa_kernel(tc, x, lora_A, lora_B, W, bias, lora_we
                 banks.append(bank)
             return banks
 
-        def c_unit(banks, engines):
+        def c_unit(banks):
             g_t = grp.tile([P, 4096], BF16, tag="grp", name="g_t", align_bytes=64)
             g_w = g_t[:].bitcast(F32)
             for c in range(4):
-                dst = g_w[:, c * 512:(c + 1) * 512].rearrange("p (k u) -> p k u", u=2)
-                src = banks[c][:].rearrange("p (u k) -> p k u", u=2)
-                if engines[c] == "s":
-                    nc.scalar.copy(out=dst, in_=src)
-                else:
-                    nc.vector.tensor_copy(out=dst, in_=src)
+                nc.scalar.copy(
+                    out=g_w[:, c * 512:(c + 1) * 512].rearrange("p (k u) -> p k u", u=2),
+                    in_=banks[c][:].rearrange("p (u k) -> p k u", u=2),
+                )
             return g_t
 
         for (src_t, codes, planes) in ((x_sb, xq, xs), (a_sb, aq, asc)):
             words = src_t[:].bitcast(F32)
             for pair in range(2):
-                banks = t_unit(words, 2 * pair)
-                g_t = c_unit(banks, "svsv")
+                g_t = c_unit(t_unit(words, 2 * pair))
                 nc.vector.quantize_mx(
                     out=codes[:, pair * 1024:(pair + 1) * 1024].bitcast(FP8X4),
                     scales=planes[:, pair * 1024:(pair + 1) * 1024],
@@ -134,16 +131,52 @@ def tile_replaced_compose_lora_pa_kernel(tc, x, lora_A, lora_B, W, bias, lora_we
         nc.vector.tensor_reduce(out=coef1[:], in_=sel[:], axis=mybir.AxisListType.X, op=ADD)
         nc.vector.tensor_scalar(out=coef[:], in0=coef1[:], scalar1=SCALE, scalar2=None, op0=MULT)
 
-        bl = bpool.tile([P, 8192], BF16, tag="b", name="bl", align_bytes=64)
-        b_w = b_sb[:].bitcast(F32).rearrange("p (n l s u) -> p l u n s", n=32, l=16, s=4, u=2)
-        bl_w = bl[:].bitcast(F32)
-        bl_v = bl_w.rearrange("p (l u n s) -> p l u n s", l=16, u=2, n=32, s=4)
-        for half in range(2):
-            for u in range(2):
-                nc.vector.tensor_copy(
-                    out=bl_v[:, :, u, half * 16:(half + 1) * 16, :],
-                    in_=b_w[:, :, u, half * 16:(half + 1) * 16, :],
+        def w_t(k):
+            return t_unit(w_sb[k // 2][:].bitcast(F32), 2 * (k % 2))
+
+        def w_cq(k, banks):
+            g_t = c_unit(banks)
+            for c in range(4):
+                o0 = (k // 2) * 2048 + c * 512 + (k % 2) * 256
+                nc.vector.quantize_mx(
+                    out=wq[:, o0:o0 + 256].bitcast(FP8X4),
+                    scales=ws[:, o0:o0 + 256],
+                    in_=g_t[:, c * 1024:(c + 1) * 1024],
                 )
+
+        def base(g, tt):
+            acc = accp.tile([P, 512], F32, tag="acc", name="acc")
+            x0 = (tt // 2) * 1024 + (tt % 2) * P
+            for c in range(4):
+                nc.tensor.matmul_mx(
+                    out=acc[:],
+                    lhsT=xq[:, x0 + c * 256:x0 + c * 256 + P].bitcast(FP8X4),
+                    lhsT_scale=xs[:, x0 + c * 256:x0 + c * 256 + P],
+                    rhs=wq[:, g * 2048 + c * 512:g * 2048 + (c + 1) * 512].bitcast(FP8X4),
+                    rhs_scale=ws[:, g * 2048 + c * 512:g * 2048 + (c + 1) * 512],
+                    start=(c == 0),
+                    stop=False,
+                )
+            return acc
+
+        def lora(g, tt, acc):
+            nc.tensor.matmul_mx(
+                out=acc[:],
+                lhsT=hq[:, tt * P:(tt + 1) * P].bitcast(FP8X4),
+                lhsT_scale=hs[:, tt * P:(tt + 1) * P],
+                rhs=bq[:, g * 512:(g + 1) * 512].bitcast(FP8X4),
+                rhs_scale=bs[:, g * 512:(g + 1) * 512],
+                start=False,
+                stop=True,
+            )
+
+        def fin(g, tt, acc):
+            o_sb = outp.tile([P, 512], F32, tag="o", name="o_sb")
+            nc.vector.tensor_tensor(out=o_sb[:], in0=acc[:], in1=bias_b[:, g * 512:(g + 1) * 512], op=ADD)
+            nc.sync.dma_start(out=out_rows[tt * P:(tt + 1) * P, g * 512:(g + 1) * 512], in_=o_sb[:])
+
+        w_cq(0, w_t(0))
+        w_cq(1, w_t(1))
 
         for tt in range(4):
             acc = accp.tile([P, 512], F32, tag="acc", name="acc")
@@ -164,76 +197,68 @@ def tile_replaced_compose_lora_pa_kernel(tc, x, lora_A, lora_B, W, bias, lora_we
                 out=hg[:, tt * 512:(tt + 1) * 512].rearrange("q (r t) -> q r t", t=4),
                 in_=acc[:].rearrange("q (t r) -> q r t", t=4),
             )
+
+        bl = bpool.tile([P, 8192], BF16, tag="b", name="bl", align_bytes=64)
+        b_w = b_sb[:].bitcast(F32).rearrange("p (n l s u) -> p l u n s", n=32, l=16, s=4, u=2)
+        bl_w = bl[:].bitcast(F32)
+        bl_v = bl_w.rearrange("p (l u n s) -> p l u n s", l=16, u=2, n=32, s=4)
+        for half in range(2):
+            for u in range(2):
+                nc.vector.tensor_copy(
+                    out=bl_v[:, :, u, half * 16:(half + 1) * 16, :],
+                    in_=b_w[:, :, u, half * 16:(half + 1) * 16, :],
+                )
         nc.vector.quantize_mx(out=hq[:].bitcast(FP8X4), scales=hs[:], in_=hg[:])
 
+        accs = [base(0, 0), base(0, 1)]
+
         bg = bpool.tile([P, 8192], BF16, tag="b", name="bg", align_bytes=64)
-        bg_v = bg[:].rearrange("q (p l a e) -> q p l a e", p=P, l=8, a=4, e=2)
+        bg_v = bg[:].bitcast(F32).rearrange("q (p l a) -> q p l a", p=P, l=8, a=4)
         for lp in range(8):
             bank = tps.tile([P, 512], F32, tag="tp", name="bankb")
             for a in range(4):
                 col = (2 * lp + a // 2) * 256 + (a % 2) * P
                 nc.tensor.transpose(bank[:, a * P:(a + 1) * P], bl_w[:, col:col + P], ident[:])
-            src = bank[:].bitcast(BF16).rearrange("q (a p e) -> q p a e", a=4, e=2)
+            src = bank[:].rearrange("q (a p) -> q p a", a=4)
             if (lp // 2) % 2 == 0:
-                nc.scalar.activation(out=bg_v[:, :, lp, :, :], in_=src, func=COPY, scale=coef[:, 0:1])
+                nc.scalar.copy(out=bg_v[:, :, lp, :], in_=src)
             else:
-                nc.vector.tensor_scalar(out=bg_v[:, :, lp, :, :], in0=src, scalar1=coef[:, 0:1], scalar2=None, op0=MULT)
-        for half in range(2):
+                nc.vector.tensor_copy(out=bg_v[:, :, lp, :], in_=src)
+
+        def b_scale_quantise(half):
+            part = bg[:, half * 4096:(half + 1) * 4096]
+            nc.vector.tensor_scalar(out=part, in0=part, scalar1=coef[:, 0:1], scalar2=None, op0=MULT)
             nc.vector.quantize_mx(
                 out=bq[:, half * 1024:(half + 1) * 1024].bitcast(FP8X4),
                 scales=bs[:, half * 1024:(half + 1) * 1024],
-                in_=bg[:, half * 4096:(half + 1) * 4096],
+                in_=part,
             )
 
-        def w_t(g, pair):
-            return t_unit(w_sb[g][:].bitcast(F32), 2 * pair)
+        banks = w_t(2)
+        b_scale_quantise(0)
+        w_cq(2, banks)
+        accs.append(base(0, 2))
+        accs.append(base(0, 3))
+        w_cq(3, w_t(3))
+        for tt in range(4):
+            lora(0, tt, accs[tt])
+        banks = w_t(4)
+        fin(0, 0, accs[0])
+        fin(0, 1, accs[1])
+        w_cq(4, banks)
+        fin(0, 2, accs[2])
+        fin(0, 3, accs[3])
+        b_scale_quantise(1)
 
-        def w_cq(g, pair, banks):
-            g_t = c_unit(banks, "sssv")
-            for c in range(4):
-                o0 = g * 2048 + c * 512 + pair * 256
-                nc.vector.quantize_mx(
-                    out=wq[:, o0:o0 + 256].bitcast(FP8X4),
-                    scales=ws[:, o0:o0 + 256],
-                    in_=g_t[:, c * 1024:(c + 1) * 1024],
-                )
-
-        def mm(g, tt):
-            acc = accp.tile([P, 512], F32, tag="acc", name="acc")
-            x0 = (tt // 2) * 1024 + (tt % 2) * P
-            for c in range(4):
-                nc.tensor.matmul_mx(
-                    out=acc[:],
-                    lhsT=xq[:, x0 + c * 256:x0 + c * 256 + P].bitcast(FP8X4),
-                    lhsT_scale=xs[:, x0 + c * 256:x0 + c * 256 + P],
-                    rhs=wq[:, g * 2048 + c * 512:g * 2048 + (c + 1) * 512].bitcast(FP8X4),
-                    rhs_scale=ws[:, g * 2048 + c * 512:g * 2048 + (c + 1) * 512],
-                    start=(c == 0),
-                    stop=False,
-                )
-            nc.tensor.matmul_mx(
-                out=acc[:],
-                lhsT=hq[:, tt * P:(tt + 1) * P].bitcast(FP8X4),
-                lhsT_scale=hs[:, tt * P:(tt + 1) * P],
-                rhs=bq[:, g * 512:(g + 1) * 512].bitcast(FP8X4),
-                rhs_scale=bs[:, g * 512:(g + 1) * 512],
-                start=False,
-                stop=True,
-            )
-            return acc
-
-        def fin(g, tt, acc):
-            o_sb = outp.tile([P, 512], F32, tag="o", name="o_sb")
-            nc.vector.tensor_tensor(out=o_sb[:], in0=acc[:], in1=bias_b[:, g * 512:(g + 1) * 512], op=ADD)
-            nc.sync.dma_start(out=out_rows[tt * P:(tt + 1) * P, g * 512:(g + 1) * 512], in_=o_sb[:])
-
-        for pair in range(2):
-            w_cq(0, pair, w_t(0, pair))
-        for g in range(4):
-            for half in range(2):
-                accs = [mm(g, 2 * half), mm(g, 2 * half + 1)]
-                banks = w_t(g + 1, half) if g < 3 else None
-                fin(g, 2 * half, accs[0])
-                fin(g, 2 * half + 1, accs[1])
-                if g < 3:
-                    w_cq(g + 1, half, banks)
+        for m in range(2, 8):
+            g = m // 2
+            accs = []
+            for tt in (2 * (m % 2), 2 * (m % 2) + 1):
+                acc = base(g, tt)
+                lora(g, tt, acc)
+                accs.append(acc)
+            banks = w_t(m + 3) if m + 3 < 8 else None
+            fin(g, 2 * (m % 2), accs[0])
+            fin(g, 2 * (m % 2) + 1, accs[1])
+            if m + 3 < 8:
+                w_cq(m + 3, banks)

@@ -7,6 +7,7 @@ F32 = mybir.dt.float32
 BF16 = mybir.dt.bfloat16
 U32 = mybir.dt.uint32
 U8 = mybir.dt.uint8
+I32 = mybir.dt.int32
 FP8X4 = mybir.dt.float8_e4m3fn_x4
 ADD = mybir.AluOpType.add
 MULT = mybir.AluOpType.mult
@@ -54,15 +55,20 @@ def tile_replaced_compose_lora_pa_kernel(tc, x, lora_A, lora_B, W, bias, lora_we
         hs = const.tile([P, 512], U8, name="hs", align_bytes=64)
         hg = const.tile([P, 2048], BF16, name="hg", align_bytes=64)
         bias_b = const.tile([P, O], BF16, name="bias_b")
-        lw_b = const.tile([P, 32], BF16, name="lw_b")
+        ones = const.tile([P, P], BF16, name="ones")
+        rows = const.tile([P, O + 64], BF16, name="rows")
         sel = const.tile([P, P], F32, name="sel")
         coef1 = const.tile([P, 1], F32, name="coef1")
         coef = const.tile([P, 1], F32, name="coef")
 
+        nc.vector.memset(rows[:].bitcast(I32), 0)
+        nc.vector.memset(ones[:], 1.0)
+        nc.scalar.dma_start(out=rows[0:1, O:O + 32], in_=lora_weights.rearrange("(o n) -> o n", o=1))
+        nc.scalar.dma_start(out=rows[0:1, 0:O], in_=bias.rearrange("(o n) -> o n", o=1))
+
         x_sb = raw.tile([P, 8192], BF16, tag="raw", name="x_sb")
         for tt in range(4):
             nc.sync.dma_start(out=x_sb[:, tt * D:(tt + 1) * D], in_=x_rows[tt * P:(tt + 1) * P, :])
-        nc.sync.dma_start(out=lw_b[:], in_=lora_weights.partition_broadcast(P))
         a_sb = raw.tile([P, 8192], BF16, tag="raw", name="a_sb")
         for half in range(2):
             nc.sync.dma_start(out=a_sb[:, half * 4096:(half + 1) * 4096], in_=a_rows[:, half * 4096:(half + 1) * 4096])
@@ -86,7 +92,6 @@ def tile_replaced_compose_lora_pa_kernel(tc, x, lora_A, lora_B, W, bias, lora_we
                 in_=b_rows[:, half * 16:(half + 1) * 16, :],
             )
         load_w(1)
-        nc.sync.dma_start(out=bias_b[:], in_=bias.partition_broadcast(P))
 
         def t_unit(words, first):
             banks = []
@@ -110,6 +115,21 @@ def tile_replaced_compose_lora_pa_kernel(tc, x, lora_A, lora_B, W, bias, lora_we
                 )
             return g_t
 
+        lw_ps = tps.tile([P, 512], F32, tag="tp", name="lw_ps")
+        nc.tensor.matmul(lw_ps[:, 0:64], lhsT=ones[:], rhs=rows[:, O:O + 64], start=True, stop=True)
+        nc.vector.tensor_tensor(
+            out=sel[:].rearrange("p (n s) -> p n s", s=4),
+            in0=ident[:].rearrange("p (n s) -> p n s", s=4),
+            in1=lw_ps[:, 0:32].unsqueeze(2).to_broadcast([P, 32, 4]),
+            op=MULT,
+        )
+        nc.vector.tensor_reduce(out=coef1[:], in_=sel[:], axis=mybir.AxisListType.X, op=ADD)
+        nc.vector.tensor_scalar(out=coef[:], in0=coef1[:], scalar1=SCALE, scalar2=None, op0=MULT)
+        for g in range(4):
+            b_ps = tps.tile([P, 512], F32, tag="tp", name="b_ps")
+            nc.tensor.matmul(b_ps[:], lhsT=ones[:], rhs=rows[:, g * 512:(g + 1) * 512], start=True, stop=True)
+            nc.vector.tensor_copy(out=bias_b[:, g * 512:(g + 1) * 512], in_=b_ps[:])
+
         for (src_t, codes, planes) in ((x_sb, xq, xs), (a_sb, aq, asc)):
             words = src_t[:].bitcast(F32)
             for pair in range(2):
@@ -121,15 +141,6 @@ def tile_replaced_compose_lora_pa_kernel(tc, x, lora_A, lora_B, W, bias, lora_we
                 )
         load_w(2)
         load_w(3)
-
-        nc.vector.tensor_tensor(
-            out=sel[:].rearrange("p (n s) -> p n s", s=4),
-            in0=ident[:].rearrange("p (n s) -> p n s", s=4),
-            in1=lw_b[:].unsqueeze(2).to_broadcast([P, 32, 4]),
-            op=MULT,
-        )
-        nc.vector.tensor_reduce(out=coef1[:], in_=sel[:], axis=mybir.AxisListType.X, op=ADD)
-        nc.vector.tensor_scalar(out=coef[:], in0=coef1[:], scalar1=SCALE, scalar2=None, op0=MULT)
 
         def w_t(k):
             return t_unit(w_sb[k // 2][:].bitcast(F32), 2 * (k % 2))

@@ -63,8 +63,8 @@ def tile_replaced_compose_lora_pa_kernel(tc, x, lora_A, lora_B, W, bias, lora_we
 
         nc.vector.memset(rows[:].bitcast(I32), 0)
         nc.vector.memset(ones[:], 1.0)
-        nc.scalar.dma_start(out=rows[0:1, O:O + 32], in_=lora_weights.rearrange("(o n) -> o n", o=1))
-        nc.scalar.dma_start(out=rows[0:1, 0:O], in_=bias.rearrange("(o n) -> o n", o=1))
+        nc.sync.dma_start(out=rows[0:1, O:O + 32], in_=lora_weights.rearrange("(o n) -> o n", o=1))
+        nc.sync.dma_start(out=rows[0:1, 0:O], in_=bias.rearrange("(o n) -> o n", o=1))
 
         x_sb = raw.tile([P, 8192], BF16, tag="raw", name="x_sb")
         for tt in range(4):
@@ -115,33 +115,6 @@ def tile_replaced_compose_lora_pa_kernel(tc, x, lora_A, lora_B, W, bias, lora_we
                 )
             return g_t
 
-        lw_ps = tps.tile([P, 512], F32, tag="tp", name="lw_ps")
-        nc.tensor.matmul(lw_ps[:, 0:64], lhsT=ones[:], rhs=rows[:, O:O + 64], start=True, stop=True)
-        nc.vector.tensor_tensor(
-            out=sel[:].rearrange("p (n s) -> p n s", s=4),
-            in0=ident[:].rearrange("p (n s) -> p n s", s=4),
-            in1=lw_ps[:, 0:32].unsqueeze(2).to_broadcast([P, 32, 4]),
-            op=MULT,
-        )
-        nc.vector.tensor_reduce(out=coef1[:], in_=sel[:], axis=mybir.AxisListType.X, op=ADD)
-        nc.vector.tensor_scalar(out=coef[:], in0=coef1[:], scalar1=SCALE, scalar2=None, op0=MULT)
-        for g in range(4):
-            b_ps = tps.tile([P, 512], F32, tag="tp", name="b_ps")
-            nc.tensor.matmul(b_ps[:], lhsT=ones[:], rhs=rows[:, g * 512:(g + 1) * 512], start=True, stop=True)
-            nc.vector.tensor_copy(out=bias_b[:, g * 512:(g + 1) * 512], in_=b_ps[:])
-
-        for (src_t, codes, planes) in ((x_sb, xq, xs), (a_sb, aq, asc)):
-            words = src_t[:].bitcast(F32)
-            for pair in range(2):
-                g_t = c_unit(t_unit(words, 2 * pair))
-                nc.vector.quantize_mx(
-                    out=codes[:, pair * 1024:(pair + 1) * 1024].bitcast(FP8X4),
-                    scales=planes[:, pair * 1024:(pair + 1) * 1024],
-                    in_=g_t[:],
-                )
-        load_w(2)
-        load_w(3)
-
         def w_t(k):
             return t_unit(w_sb[k // 2][:].bitcast(F32), 2 * (k % 2))
 
@@ -186,8 +159,43 @@ def tile_replaced_compose_lora_pa_kernel(tc, x, lora_A, lora_B, W, bias, lora_we
             nc.vector.tensor_tensor(out=o_sb[:], in0=acc[:], in1=bias_b[:, g * 512:(g + 1) * 512], op=ADD)
             nc.sync.dma_start(out=out_rows[tt * P:(tt + 1) * P, g * 512:(g + 1) * 512], in_=o_sb[:])
 
-        w_cq(0, w_t(0))
-        w_cq(1, w_t(1))
+        def spread(i):
+            ps = accp.tile([P, 512], F32, tag="acc", name="ps")
+            if i == 0:
+                nc.tensor.matmul(ps[:, 0:64], lhsT=ones[:], rhs=rows[:, O:O + 64], start=True, stop=True)
+                nc.vector.tensor_tensor(
+                    out=sel[:].rearrange("p (n s) -> p n s", s=4),
+                    in0=ident[:].rearrange("p (n s) -> p n s", s=4),
+                    in1=ps[:, 0:32].unsqueeze(2).to_broadcast([P, 32, 4]),
+                    op=MULT,
+                )
+                nc.vector.tensor_reduce(out=coef1[:], in_=sel[:], axis=mybir.AxisListType.X, op=ADD)
+                nc.vector.tensor_scalar(out=coef[:], in0=coef1[:], scalar1=SCALE, scalar2=None, op0=MULT)
+            else:
+                cols = slice((i - 1) * 512, i * 512)
+                nc.tensor.matmul(ps[:], lhsT=ones[:], rhs=rows[:, cols], start=True, stop=True)
+                nc.vector.tensor_copy(out=bias_b[:, cols], in_=ps[:])
+
+        for i in range(6):
+            pair = i % 2
+            if i < 4:
+                src_t, codes, planes = ((x_sb, xq, xs), (a_sb, aq, asc))[i // 2]
+                banks = t_unit(src_t[:].bitcast(F32), 2 * pair)
+            else:
+                banks = w_t(pair)
+            if i < 5:
+                spread(i)
+            if i < 4:
+                g_t = c_unit(banks)
+                nc.vector.quantize_mx(
+                    out=codes[:, pair * 1024:(pair + 1) * 1024].bitcast(FP8X4),
+                    scales=planes[:, pair * 1024:(pair + 1) * 1024],
+                    in_=g_t[:],
+                )
+            else:
+                w_cq(pair, banks)
+        load_w(2)
+        load_w(3)
 
         for tt in range(4):
             acc = accp.tile([P, 512], F32, tag="acc", name="acc")

@@ -7,7 +7,6 @@ F32 = mybir.dt.float32
 BF16 = mybir.dt.bfloat16
 U32 = mybir.dt.uint32
 U8 = mybir.dt.uint8
-I32 = mybir.dt.int32
 FP8X4 = mybir.dt.float8_e4m3fn_x4
 ADD = mybir.AluOpType.add
 MULT = mybir.AluOpType.mult
@@ -55,20 +54,15 @@ def tile_replaced_compose_lora_pa_kernel(tc, x, lora_A, lora_B, W, bias, lora_we
         hs = const.tile([P, 512], U8, name="hs", align_bytes=64)
         hg = const.tile([P, 2048], BF16, name="hg", align_bytes=64)
         bias_b = const.tile([P, O], BF16, name="bias_b")
-        ones = const.tile([P, P], BF16, name="ones")
-        rows = const.tile([P, O + 64], BF16, name="rows")
+        lw_b = const.tile([P, 32], BF16, name="lw_b")
         sel = const.tile([P, P], F32, name="sel")
         coef1 = const.tile([P, 1], F32, name="coef1")
         coef = const.tile([P, 1], F32, name="coef")
 
-        nc.vector.memset(rows[:].bitcast(I32), 0)
-        nc.vector.memset(ones[:], 1.0)
-        nc.sync.dma_start(out=rows[0:1, O:O + 32], in_=lora_weights.rearrange("(o n) -> o n", o=1))
-        nc.sync.dma_start(out=rows[0:1, 0:O], in_=bias.rearrange("(o n) -> o n", o=1))
-
         x_sb = raw.tile([P, 8192], BF16, tag="raw", name="x_sb")
         for tt in range(4):
             nc.sync.dma_start(out=x_sb[:, tt * D:(tt + 1) * D], in_=x_rows[tt * P:(tt + 1) * P, :])
+        nc.sync.dma_start(out=lw_b[:], in_=lora_weights.partition_broadcast(P))
         a_sb = raw.tile([P, 8192], BF16, tag="raw", name="a_sb")
         for half in range(2):
             nc.sync.dma_start(out=a_sb[:, half * 4096:(half + 1) * 4096], in_=a_rows[:, half * 4096:(half + 1) * 4096])
@@ -92,6 +86,7 @@ def tile_replaced_compose_lora_pa_kernel(tc, x, lora_A, lora_B, W, bias, lora_we
                 in_=b_rows[:, half * 16:(half + 1) * 16, :],
             )
         load_w(1)
+        nc.sync.dma_start(out=bias_b[:], in_=bias.partition_broadcast(P))
 
         def t_unit(words, first):
             banks = []
@@ -115,11 +110,31 @@ def tile_replaced_compose_lora_pa_kernel(tc, x, lora_A, lora_B, W, bias, lora_we
                 )
             return g_t
 
+        for (src_t, codes, planes) in ((x_sb, xq, xs), (a_sb, aq, asc)):
+            words = src_t[:].bitcast(F32)
+            for pair in range(2):
+                g_t = c_unit(t_unit(words, 2 * pair))
+                nc.vector.quantize_mx(
+                    out=codes[:, pair * 1024:(pair + 1) * 1024].bitcast(FP8X4),
+                    scales=planes[:, pair * 1024:(pair + 1) * 1024],
+                    in_=g_t[:],
+                )
+        load_w(2)
+        load_w(3)
+
+        nc.vector.tensor_tensor(
+            out=sel[:].rearrange("p (n s) -> p n s", s=4),
+            in0=ident[:].rearrange("p (n s) -> p n s", s=4),
+            in1=lw_b[:].unsqueeze(2).to_broadcast([P, 32, 4]),
+            op=MULT,
+        )
+        nc.vector.tensor_reduce(out=coef1[:], in_=sel[:], axis=mybir.AxisListType.X, op=ADD)
+        nc.vector.tensor_scalar(out=coef[:], in0=coef1[:], scalar1=SCALE, scalar2=None, op0=MULT)
+
         def w_t(k):
             return t_unit(w_sb[k // 2][:].bitcast(F32), 2 * (k % 2))
 
-        def w_cq(k, banks):
-            g_t = c_unit(banks)
+        def w_q(k, g_t):
             for c in range(4):
                 o0 = (k // 2) * 2048 + c * 512 + (k % 2) * 256
                 nc.vector.quantize_mx(
@@ -127,6 +142,9 @@ def tile_replaced_compose_lora_pa_kernel(tc, x, lora_A, lora_B, W, bias, lora_we
                     scales=ws[:, o0:o0 + 256],
                     in_=g_t[:, c * 1024:(c + 1) * 1024],
                 )
+
+        def w_cq(k, banks):
+            w_q(k, c_unit(banks))
 
         def base(g, tt):
             acc = accp.tile([P, 512], F32, tag="acc", name="acc")
@@ -159,52 +177,27 @@ def tile_replaced_compose_lora_pa_kernel(tc, x, lora_A, lora_B, W, bias, lora_we
             nc.vector.tensor_tensor(out=o_sb[:], in0=acc[:], in1=bias_b[:, g * 512:(g + 1) * 512], op=ADD)
             nc.sync.dma_start(out=out_rows[tt * P:(tt + 1) * P, g * 512:(g + 1) * 512], in_=o_sb[:])
 
-        def spread(i):
-            ps = accp.tile([P, 512], F32, tag="acc", name="ps")
-            if i == 0:
-                nc.tensor.matmul(ps[:, 0:64], lhsT=ones[:], rhs=rows[:, O:O + 64], start=True, stop=True)
-                nc.vector.tensor_tensor(
-                    out=sel[:].rearrange("p (n s) -> p n s", s=4),
-                    in0=ident[:].rearrange("p (n s) -> p n s", s=4),
-                    in1=ps[:, 0:32].unsqueeze(2).to_broadcast([P, 32, 4]),
-                    op=MULT,
-                )
-                nc.vector.tensor_reduce(out=coef1[:], in_=sel[:], axis=mybir.AxisListType.X, op=ADD)
-                nc.vector.tensor_scalar(out=coef[:], in0=coef1[:], scalar1=SCALE, scalar2=None, op0=MULT)
-            else:
-                cols = slice((i - 1) * 512, i * 512)
-                nc.tensor.matmul(ps[:], lhsT=ones[:], rhs=rows[:, cols], start=True, stop=True)
-                nc.vector.tensor_copy(out=bias_b[:, cols], in_=ps[:])
+        bl = bpool.tile([P, 8192], BF16, tag="b", name="bl", align_bytes=64)
+        b_w = b_sb[:].bitcast(F32).rearrange("p (n l s u) -> p l u n s", n=32, l=16, s=4, u=2)
+        bl_w = bl[:].bitcast(F32)
+        bl_v = bl_w.rearrange("p (l u n s) -> p l u n s", l=16, u=2, n=32, s=4)
 
-        for i in range(6):
-            pair = i % 2
-            if i < 4:
-                src_t, codes, planes = ((x_sb, xq, xs), (a_sb, aq, asc))[i // 2]
-                banks = t_unit(src_t[:].bitcast(F32), 2 * pair)
-            else:
-                banks = w_t(pair)
-            if i < 5:
-                spread(i)
-            if i < 4:
-                g_t = c_unit(banks)
-                nc.vector.quantize_mx(
-                    out=codes[:, pair * 1024:(pair + 1) * 1024].bitcast(FP8X4),
-                    scales=planes[:, pair * 1024:(pair + 1) * 1024],
-                    in_=g_t[:],
+        def sort_b(half):
+            for u in range(2):
+                nc.vector.tensor_copy(
+                    out=bl_v[:, :, u, half * 16:(half + 1) * 16, :],
+                    in_=b_w[:, :, u, half * 16:(half + 1) * 16, :],
                 )
-            else:
-                w_cq(pair, banks)
-        load_w(2)
-        load_w(3)
 
-        for tt in range(4):
-            acc = accp.tile([P, 512], F32, tag="acc", name="acc")
+        h_acc = []
+
+        def h_groups(tt, ts):
             x0 = (tt // 2) * 1024 + (tt % 2) * P
-            for t in range(4):
+            for t in ts:
                 a0 = (t // 2) * 1024 + (t % 2) * P
                 for c in range(4):
                     nc.tensor.matmul_mx(
-                        out=acc[:, t * P:(t + 1) * P],
+                        out=h_acc[tt][:, t * P:(t + 1) * P],
                         lhsT=aq[:, a0 + c * 256:a0 + c * 256 + P].bitcast(FP8X4),
                         lhsT_scale=asc[:, a0 + c * 256:a0 + c * 256 + P],
                         rhs=xq[:, x0 + c * 256:x0 + c * 256 + P].bitcast(FP8X4),
@@ -212,21 +205,22 @@ def tile_replaced_compose_lora_pa_kernel(tc, x, lora_A, lora_B, W, bias, lora_we
                         start=(c == 0),
                         stop=(c == 3),
                     )
+
+        w_cq(0, w_t(0))
+        for tt in range(4):
+            acc = accp.tile([P, 512], F32, tag="acc", name="acc")
+            h_acc.append(acc)
+            h_groups(tt, (0, 1))
+        g_t = c_unit(w_t(1))
+        sort_b(0)
+        w_q(1, g_t)
+        for tt in range(4):
+            h_groups(tt, (2, 3))
             nc.scalar.copy(
                 out=hg[:, tt * 512:(tt + 1) * 512].rearrange("q (r t) -> q r t", t=4),
-                in_=acc[:].rearrange("q (t r) -> q r t", t=4),
+                in_=h_acc[tt][:].rearrange("q (t r) -> q r t", t=4),
             )
-
-        bl = bpool.tile([P, 8192], BF16, tag="b", name="bl", align_bytes=64)
-        b_w = b_sb[:].bitcast(F32).rearrange("p (n l s u) -> p l u n s", n=32, l=16, s=4, u=2)
-        bl_w = bl[:].bitcast(F32)
-        bl_v = bl_w.rearrange("p (l u n s) -> p l u n s", l=16, u=2, n=32, s=4)
-        for half in range(2):
-            for u in range(2):
-                nc.vector.tensor_copy(
-                    out=bl_v[:, :, u, half * 16:(half + 1) * 16, :],
-                    in_=b_w[:, :, u, half * 16:(half + 1) * 16, :],
-                )
+        sort_b(1)
         nc.vector.quantize_mx(out=hq[:].bitcast(FP8X4), scales=hs[:], in_=hg[:])
 
         accs = [base(0, 0), base(0, 1)]
@@ -253,10 +247,10 @@ def tile_replaced_compose_lora_pa_kernel(tc, x, lora_A, lora_B, W, bias, lora_we
                 in_=part,
             )
 
+        accs.append(base(0, 2))
         banks = w_t(2)
         b_scale_quantise(0)
         w_cq(2, banks)
-        accs.append(base(0, 2))
         accs.append(base(0, 3))
         w_cq(3, w_t(3))
         for tt in range(4):

@@ -10,21 +10,28 @@ U8 = mybir.dt.uint8
 FP8X4 = mybir.dt.float8_e4m3fn_x4
 ADD = mybir.AluOpType.add
 MULT = mybir.AluOpType.mult
-COPY = mybir.ActivationFunctionType.Copy
 
 P = 128
-TOK = 512
-D = 2048
-O = 2048
-NR = 512
+TOKENS = 512
+D_IN = 2048
+D_OUT = 2048
+ADAPTERS = 32
+RANK = 16
+K_LORA = ADAPTERS * RANK
 SCALE = 2.0
-FLOPS = 2 * TOK * D * O + 2 * TOK * D * NR + 2 * TOK * NR * O
+PASSES = D_IN // 512
+GROUP = 512
+UNIT = 256
+W_UNITS = D_OUT // UNIT
+B_RUN = 16 * RANK
+AHEAD = 3
+FLOPS = 2 * TOKENS * D_IN * D_OUT + 2 * TOKENS * D_IN * K_LORA + 2 * TOKENS * K_LORA * D_OUT
 
 
 def tile_replaced_compose_lora_pa_kernel(tc, x, lora_A, lora_B, W, bias, lora_weights, out):
     nc = tc.nc
     with ExitStack() as ctx:
-        const = ctx.enter_context(tc.tile_pool(name="const", bufs=1))
+        keep = ctx.enter_context(tc.tile_pool(name="keep", bufs=1))
         raw = ctx.enter_context(tc.tile_pool(name="raw", bufs=4))
         bpool = ctx.enter_context(tc.tile_pool(name="bpool", bufs=2))
         grp = ctx.enter_context(tc.tile_pool(name="grp", bufs=3))
@@ -33,245 +40,229 @@ def tile_replaced_compose_lora_pa_kernel(tc, x, lora_A, lora_B, W, bias, lora_we
         accp = ctx.enter_context(tc.psum_pool(name="accp", bufs=4))
         ctx.enter_context(tc.manual_schedule())
 
-        x_rows = x.rearrange("b s d -> (b s) d")
-        a_rows = lora_A.rearrange("n r d -> (n r) d").rearrange("(q t) d -> q (t d)", t=4)
+        x_rows = x.rearrange("b s d -> (b s) d").rearrange("(i p) d -> p i d", p=P)
+        a_rows = lora_A.rearrange("n r d -> (n r) d").rearrange("(q t) d -> q t d", t=4)
+        w_rows = W.rearrange("(i p) d -> p i d", p=P)
         b_rows = lora_B.rearrange("n (p l) r -> p n (l r)", l=16)
-        w_rows = W.rearrange("(a p) d -> p a d", p=P)
         out_rows = out.rearrange("b s o -> (b s) o")
 
-        ident = const.tile([P, P], F32, name="ident")
+        ident = keep.tile([P, P], F32, name="ident")
         make_identity(nc, ident[:])
 
-        xq = const.tile([P, 2048], U32, name="xq", align_bytes=64)
-        xs = const.tile([P, 2048], U8, name="xs", align_bytes=64)
-        aq = const.tile([P, 2048], U32, name="aq", align_bytes=64)
-        asc = const.tile([P, 2048], U8, name="asc", align_bytes=64)
-        wq = const.tile([P, 8192], U32, name="wq", align_bytes=64)
-        ws = const.tile([P, 8192], U8, name="ws", align_bytes=64)
-        bq = const.tile([P, 2048], U32, name="bq", align_bytes=64)
-        bs = const.tile([P, 2048], U8, name="bs", align_bytes=64)
-        hq = const.tile([P, 512], U32, name="hq", align_bytes=64)
-        hs = const.tile([P, 512], U8, name="hs", align_bytes=64)
-        hg = const.tile([P, 2048], BF16, name="hg", align_bytes=64)
-        bias_b = const.tile([P, O], BF16, name="bias_b")
-        lw_b = const.tile([P, 32], BF16, name="lw_b")
-        sel = const.tile([P, P], F32, name="sel")
-        coef1 = const.tile([P, 1], F32, name="coef1")
-        coef = const.tile([P, 1], F32, name="coef")
+        x_codes = keep.tile([P, PASSES, GROUP], U32, name="x_codes", align_bytes=64)
+        x_scales = keep.tile([P, PASSES, GROUP], U8, name="x_scales", align_bytes=64)
+        a_codes = keep.tile([P, PASSES, GROUP], U32, name="a_codes", align_bytes=64)
+        a_scales = keep.tile([P, PASSES, GROUP], U8, name="a_scales", align_bytes=64)
+        w_codes = keep.tile([P, D_OUT // GROUP, PASSES, GROUP], U32, name="w_codes", align_bytes=64)
+        w_scales = keep.tile([P, D_OUT // GROUP, PASSES, GROUP], U8, name="w_scales", align_bytes=64)
+        b_codes = keep.tile([P, D_OUT], U32, name="b_codes", align_bytes=64)
+        b_scales = keep.tile([P, D_OUT], U8, name="b_scales", align_bytes=64)
+        h_codes = keep.tile([P, TOKENS], U32, name="h_codes", align_bytes=64)
+        h_scales = keep.tile([P, TOKENS], U8, name="h_scales", align_bytes=64)
+        h_bf = keep.tile([P, TOKENS * 4], BF16, name="h_bf", align_bytes=64)
+        bias_all = keep.tile([P, D_OUT], BF16, name="bias_all")
+        lw_all = keep.tile([P, ADAPTERS], BF16, name="lw_all")
+        picked = keep.tile([P, P], F32, name="picked")
+        lw_own = keep.tile([P, 1], F32, name="lw_own")
+        coef = keep.tile([P, 1], F32, name="coef")
 
-        x_sb = raw.tile([P, 8192], BF16, tag="raw", name="x_sb")
-        for tt in range(4):
-            nc.sync.dma_start(out=x_sb[:, tt * D:(tt + 1) * D], in_=x_rows[tt * P:(tt + 1) * P, :])
-        nc.sync.dma_start(out=lw_b[:], in_=lora_weights.partition_broadcast(P))
-        a_sb = raw.tile([P, 8192], BF16, tag="raw", name="a_sb")
-        for half in range(2):
-            nc.sync.dma_start(out=a_sb[:, half * 4096:(half + 1) * 4096], in_=a_rows[:, half * 4096:(half + 1) * 4096])
+        def load_group(rows, first, name):
+            group = raw.tile([P, 4 * D_IN], BF16, tag="raw", name=name)
+            for i in range(4):
+                nc.sync.dma_start(out=group[:, i * D_IN:(i + 1) * D_IN], in_=rows[:, first + i, :])
+            return group
 
-        w_sb = []
-
-        def load_w(g):
-            w_t = raw.tile([P, 8192], BF16, tag="raw", name="w_sb%d" % g)
-            for half in range(2):
-                nc.sync.dma_start(
-                    out=w_t[:, half * 4096:(half + 1) * 4096].rearrange("p (a d) -> p a d", a=2),
-                    in_=w_rows[:, 4 * g + 2 * half:4 * g + 2 * half + 2, :],
-                )
-            w_sb.append(w_t)
-
-        load_w(0)
-        b_sb = bpool.tile([P, 8192], BF16, tag="b", name="b_sb", align_bytes=64)
+        x_raw = load_group(x_rows, 0, "x_raw")
+        nc.sync.dma_start(out=lw_all[:], in_=lora_weights.partition_broadcast(P))
+        a_raw = load_group(a_rows, 0, "a_raw")
+        w_raw = [load_group(w_rows, 0, "w_raw0")]
+        b_raw = bpool.tile([P, ADAPTERS * B_RUN], BF16, tag="b", name="b_raw", align_bytes=64)
         for half in range(2):
             nc.sync.dma_start(
-                out=b_sb[:, half * 4096:(half + 1) * 4096].rearrange("p (n k) -> p n k", k=256),
+                out=b_raw[:, half * 4096:(half + 1) * 4096].rearrange("p (n k) -> p n k", k=B_RUN),
                 in_=b_rows[:, half * 16:(half + 1) * 16, :],
             )
-        load_w(1)
-        nc.sync.dma_start(out=bias_b[:], in_=bias.partition_broadcast(P))
+        w_raw.append(load_group(w_rows, 4, "w_raw1"))
+        nc.sync.dma_start(out=bias_all[:], in_=bias.partition_broadcast(P))
 
-        def t_unit(words, first):
+        def transpose_unit(group, unit):
+            words = group[:].bitcast(F32).rearrange("p (i w) -> p i w", i=4)
             banks = []
-            for c in range(4):
-                bank = tps.tile([P, 512], F32, tag="tp", name="bank")
-                for u in range(2):
-                    for i in range(2):
-                        j = 2 * c + u
-                        col = (first + i) * 1024 + j * P
-                        nc.tensor.transpose(bank[:, (2 * u + i) * P:(2 * u + i + 1) * P], words[:, col:col + P], ident[:])
-                banks.append(bank)
+            for i in (2 * unit, 2 * unit + 1):
+                for b in range(2):
+                    bank = tps.tile([P, 512], F32, tag="tp", name="bank")
+                    for u in range(2):
+                        for c in range(2):
+                            first = (2 * (2 * b + c) + u) * P
+                            nc.tensor.transpose(
+                                bank[:, (2 * u + c) * P:(2 * u + c + 1) * P], words[:, i, first:first + P], ident[:]
+                            )
+                    banks.append(bank)
             return banks
 
-        def c_unit(banks):
-            g_t = grp.tile([P, 4096], BF16, tag="grp", name="g_t", align_bytes=64)
-            g_w = g_t[:].bitcast(F32)
-            for c in range(4):
-                nc.scalar.copy(
-                    out=g_w[:, c * 512:(c + 1) * 512].rearrange("p (k u) -> p k u", u=2),
-                    in_=banks[c][:].rearrange("p (u k) -> p k u", u=2),
-                )
-            return g_t
+        def regroup_unit(banks):
+            grouped = grp.tile([P, PASSES * UNIT * 4], BF16, tag="grp", name="grouped", align_bytes=64)
+            words = grouped[:].bitcast(F32).rearrange("p (c r u) -> p c r u", c=PASSES, u=2)
+            for i in range(2):
+                for b in range(2):
+                    nc.scalar.copy(
+                        out=words[:, 2 * b:2 * b + 2, i * P:(i + 1) * P, :],
+                        in_=banks[2 * i + b][:].rearrange("p (u c r) -> p c r u", u=2, c=2),
+                    )
+            return grouped
 
-        for (src_t, codes, planes) in ((x_sb, xq, xs), (a_sb, aq, asc)):
-            words = src_t[:].bitcast(F32)
-            for pair in range(2):
-                g_t = c_unit(t_unit(words, 2 * pair))
+        def quantise_unit(grouped, unit, codes, scales):
+            rows = slice(unit * UNIT, (unit + 1) * UNIT)
+            for c in range(PASSES):
                 nc.vector.quantize_mx(
-                    out=codes[:, pair * 1024:(pair + 1) * 1024].bitcast(FP8X4),
-                    scales=planes[:, pair * 1024:(pair + 1) * 1024],
-                    in_=g_t[:],
-                )
-        load_w(2)
-        load_w(3)
-
-        nc.vector.tensor_tensor(
-            out=sel[:].rearrange("p (n s) -> p n s", s=4),
-            in0=ident[:].rearrange("p (n s) -> p n s", s=4),
-            in1=lw_b[:].unsqueeze(2).to_broadcast([P, 32, 4]),
-            op=MULT,
-        )
-        nc.vector.tensor_reduce(out=coef1[:], in_=sel[:], axis=mybir.AxisListType.X, op=ADD)
-        nc.vector.tensor_scalar(out=coef[:], in0=coef1[:], scalar1=SCALE, scalar2=None, op0=MULT)
-
-        def w_t(k):
-            return t_unit(w_sb[k // 2][:].bitcast(F32), 2 * (k % 2))
-
-        def w_q(k, g_t):
-            for c in range(4):
-                o0 = (k // 2) * 2048 + c * 512 + (k % 2) * 256
-                nc.vector.quantize_mx(
-                    out=wq[:, o0:o0 + 256].bitcast(FP8X4),
-                    scales=ws[:, o0:o0 + 256],
-                    in_=g_t[:, c * 1024:(c + 1) * 1024],
+                    out=codes[:, c, rows].bitcast(FP8X4),
+                    scales=scales[:, c, rows],
+                    in_=grouped[:, c * UNIT * 4:(c + 1) * UNIT * 4],
                 )
 
-        def w_cq(k, banks):
-            w_q(k, c_unit(banks))
+        def transpose_w(k):
+            return transpose_unit(w_raw[k // 2], k % 2)
 
-        def base(g, tt):
-            acc = accp.tile([P, 512], F32, tag="acc", name="acc")
-            x0 = (tt // 2) * 1024 + (tt % 2) * P
-            for c in range(4):
+        def finish_w(k, banks):
+            quantise_unit(regroup_unit(banks), k % 2, w_codes[:, k // 2, :, :], w_scales[:, k // 2, :, :])
+
+        h_banks = []
+
+        def h_groups(tt, ts):
+            tokens = slice(tt * P, (tt + 1) * P)
+            for t in ts:
+                for c in range(PASSES):
+                    nc.tensor.matmul_mx(
+                        out=h_banks[tt][:, t * P:(t + 1) * P],
+                        lhsT=a_codes[:, c, t * P:(t + 1) * P].bitcast(FP8X4),
+                        lhsT_scale=a_scales[:, c, t * P:(t + 1) * P],
+                        rhs=x_codes[:, c, tokens].bitcast(FP8X4),
+                        rhs_scale=x_scales[:, c, tokens],
+                        start=(c == 0),
+                        stop=(c == PASSES - 1),
+                    )
+
+        b_sorted = bpool.tile([P, ADAPTERS * B_RUN], BF16, tag="b", name="b_sorted", align_bytes=64)
+        b_from = b_raw[:].bitcast(F32).rearrange("p (n l s u) -> p l u n s", n=ADAPTERS, l=16, s=4, u=2)
+        b_words = b_sorted[:].bitcast(F32)
+        b_to = b_words.rearrange("p (l u n s) -> p l u n s", l=16, u=2, n=ADAPTERS, s=4)
+
+        def sort_b(half):
+            adapters = slice(half * 16, (half + 1) * 16)
+            for u in range(2):
+                nc.vector.tensor_copy(out=b_to[:, :, u, adapters, :], in_=b_from[:, :, u, adapters, :])
+
+        def scale_quantise_b(b_bf, half):
+            part = b_bf[:, half * 4096:(half + 1) * 4096]
+            nc.vector.tensor_scalar(out=part, in0=part, scalar1=coef[:, 0:1], scalar2=None, op0=MULT)
+            nc.vector.quantize_mx(
+                out=b_codes[:, half * 1024:(half + 1) * 1024].bitcast(FP8X4),
+                scales=b_scales[:, half * 1024:(half + 1) * 1024],
+                in_=part,
+            )
+
+        def base_passes(g, tt):
+            acc = accp.tile([P, GROUP], F32, tag="acc", name="acc")
+            tokens = slice(tt * P, (tt + 1) * P)
+            for c in range(PASSES):
                 nc.tensor.matmul_mx(
                     out=acc[:],
-                    lhsT=xq[:, x0 + c * 256:x0 + c * 256 + P].bitcast(FP8X4),
-                    lhsT_scale=xs[:, x0 + c * 256:x0 + c * 256 + P],
-                    rhs=wq[:, g * 2048 + c * 512:g * 2048 + (c + 1) * 512].bitcast(FP8X4),
-                    rhs_scale=ws[:, g * 2048 + c * 512:g * 2048 + (c + 1) * 512],
+                    lhsT=x_codes[:, c, tokens].bitcast(FP8X4),
+                    lhsT_scale=x_scales[:, c, tokens],
+                    rhs=w_codes[:, g, c, :].bitcast(FP8X4),
+                    rhs_scale=w_scales[:, g, c, :],
                     start=(c == 0),
                     stop=False,
                 )
             return acc
 
-        def lora(g, tt, acc):
+        def adapter_pass(g, tt, acc):
             nc.tensor.matmul_mx(
                 out=acc[:],
-                lhsT=hq[:, tt * P:(tt + 1) * P].bitcast(FP8X4),
-                lhsT_scale=hs[:, tt * P:(tt + 1) * P],
-                rhs=bq[:, g * 512:(g + 1) * 512].bitcast(FP8X4),
-                rhs_scale=bs[:, g * 512:(g + 1) * 512],
+                lhsT=h_codes[:, tt * P:(tt + 1) * P].bitcast(FP8X4),
+                lhsT_scale=h_scales[:, tt * P:(tt + 1) * P],
+                rhs=b_codes[:, g * GROUP:(g + 1) * GROUP].bitcast(FP8X4),
+                rhs_scale=b_scales[:, g * GROUP:(g + 1) * GROUP],
                 start=False,
                 stop=True,
             )
 
-        def fin(g, tt, acc):
-            o_sb = outp.tile([P, 512], F32, tag="o", name="o_sb")
-            nc.vector.tensor_tensor(out=o_sb[:], in0=acc[:], in1=bias_b[:, g * 512:(g + 1) * 512], op=ADD)
-            nc.sync.dma_start(out=out_rows[tt * P:(tt + 1) * P, g * 512:(g + 1) * 512], in_=o_sb[:])
+        def add_bias_store(g, tt, acc):
+            result = outp.tile([P, GROUP], F32, tag="o", name="result")
+            nc.vector.tensor_tensor(out=result[:], in0=acc[:], in1=bias_all[:, g * GROUP:(g + 1) * GROUP], op=ADD)
+            nc.sync.dma_start(out=out_rows[tt * P:(tt + 1) * P, g * GROUP:(g + 1) * GROUP], in_=result[:])
 
-        bl = bpool.tile([P, 8192], BF16, tag="b", name="bl", align_bytes=64)
-        b_w = b_sb[:].bitcast(F32).rearrange("p (n l s u) -> p l u n s", n=32, l=16, s=4, u=2)
-        bl_w = bl[:].bitcast(F32)
-        bl_v = bl_w.rearrange("p (l u n s) -> p l u n s", l=16, u=2, n=32, s=4)
+        for group, codes, scales in ((x_raw, x_codes, x_scales), (a_raw, a_codes, a_scales)):
+            for unit in range(2):
+                quantise_unit(regroup_unit(transpose_unit(group, unit)), unit, codes, scales)
+        w_raw.append(load_group(w_rows, 8, "w_raw2"))
+        w_raw.append(load_group(w_rows, 12, "w_raw3"))
 
-        def sort_b(half):
-            for u in range(2):
-                nc.vector.tensor_copy(
-                    out=bl_v[:, :, u, half * 16:(half + 1) * 16, :],
-                    in_=b_w[:, :, u, half * 16:(half + 1) * 16, :],
-                )
+        nc.vector.tensor_tensor(
+            out=picked[:].rearrange("p (n s) -> p n s", s=4),
+            in0=ident[:].rearrange("p (n s) -> p n s", s=4),
+            in1=lw_all[:].unsqueeze(2).to_broadcast([P, ADAPTERS, 4]),
+            op=MULT,
+        )
+        nc.vector.tensor_reduce(out=lw_own[:], in_=picked[:], axis=mybir.AxisListType.X, op=ADD)
+        nc.vector.tensor_scalar(out=coef[:], in0=lw_own[:], scalar1=SCALE, scalar2=None, op0=MULT)
 
-        h_acc = []
-
-        def h_groups(tt, ts):
-            x0 = (tt // 2) * 1024 + (tt % 2) * P
-            for t in ts:
-                a0 = (t // 2) * 1024 + (t % 2) * P
-                for c in range(4):
-                    nc.tensor.matmul_mx(
-                        out=h_acc[tt][:, t * P:(t + 1) * P],
-                        lhsT=aq[:, a0 + c * 256:a0 + c * 256 + P].bitcast(FP8X4),
-                        lhsT_scale=asc[:, a0 + c * 256:a0 + c * 256 + P],
-                        rhs=xq[:, x0 + c * 256:x0 + c * 256 + P].bitcast(FP8X4),
-                        rhs_scale=xs[:, x0 + c * 256:x0 + c * 256 + P],
-                        start=(c == 0),
-                        stop=(c == 3),
-                    )
-
-        w_cq(0, w_t(0))
+        finish_w(0, transpose_w(0))
         for tt in range(4):
-            acc = accp.tile([P, 512], F32, tag="acc", name="acc")
-            h_acc.append(acc)
+            h_bank = accp.tile([P, 512], F32, tag="acc", name="h_bank")
+            h_banks.append(h_bank)
             h_groups(tt, (0, 1))
-        g_t = c_unit(w_t(1))
+        grouped = regroup_unit(transpose_w(1))
         sort_b(0)
-        w_q(1, g_t)
+        quantise_unit(grouped, 1, w_codes[:, 0, :, :], w_scales[:, 0, :, :])
         for tt in range(4):
             h_groups(tt, (2, 3))
             nc.scalar.copy(
-                out=hg[:, tt * 512:(tt + 1) * 512].rearrange("q (r t) -> q r t", t=4),
-                in_=h_acc[tt][:].rearrange("q (t r) -> q r t", t=4),
+                out=h_bf[:, tt * 512:(tt + 1) * 512].rearrange("q (r t) -> q r t", t=4),
+                in_=h_banks[tt][:].rearrange("q (t r) -> q r t", t=4),
             )
         sort_b(1)
-        nc.vector.quantize_mx(out=hq[:].bitcast(FP8X4), scales=hs[:], in_=hg[:])
+        nc.vector.quantize_mx(out=h_codes[:].bitcast(FP8X4), scales=h_scales[:], in_=h_bf[:])
 
-        accs = [base(0, 0), base(0, 1)]
+        accs = [base_passes(0, 0), base_passes(0, 1)]
 
-        bg = bpool.tile([P, 8192], BF16, tag="b", name="bg", align_bytes=64)
-        bg_v = bg[:].bitcast(F32).rearrange("q (p l a) -> q p l a", p=P, l=8, a=4)
-        for lp in range(8):
-            bank = tps.tile([P, 512], F32, tag="tp", name="bankb")
+        b_bf = bpool.tile([P, D_OUT * 4], BF16, tag="b", name="b_bf", align_bytes=64)
+        b_out = b_bf[:].bitcast(F32).rearrange("q (p j a) -> q p j a", p=P, j=8, a=4)
+        for j in range(8):
+            bank = tps.tile([P, 512], F32, tag="tp", name="b_bank")
             for a in range(4):
-                col = (2 * lp + a // 2) * 256 + (a % 2) * P
-                nc.tensor.transpose(bank[:, a * P:(a + 1) * P], bl_w[:, col:col + P], ident[:])
-            src = bank[:].rearrange("q (a p) -> q p a", a=4)
-            if (lp // 2) % 2 == 0:
-                nc.scalar.copy(out=bg_v[:, :, lp, :], in_=src)
+                nc.tensor.transpose(bank[:, a * P:(a + 1) * P], b_words[:, (4 * j + a) * P:(4 * j + a + 1) * P], ident[:])
+            if (j // 2) % 2 == 0:
+                nc.scalar.copy(out=b_out[:, :, j, :], in_=bank[:].rearrange("q (a p) -> q p a", a=4))
             else:
-                nc.vector.tensor_copy(out=bg_v[:, :, lp, :], in_=src)
+                nc.vector.tensor_copy(out=b_out[:, :, j, :], in_=bank[:].rearrange("q (a p) -> q p a", a=4))
 
-        def b_scale_quantise(half):
-            part = bg[:, half * 4096:(half + 1) * 4096]
-            nc.vector.tensor_scalar(out=part, in0=part, scalar1=coef[:, 0:1], scalar2=None, op0=MULT)
-            nc.vector.quantize_mx(
-                out=bq[:, half * 1024:(half + 1) * 1024].bitcast(FP8X4),
-                scales=bs[:, half * 1024:(half + 1) * 1024],
-                in_=part,
-            )
-
-        accs.append(base(0, 2))
-        banks = w_t(2)
-        b_scale_quantise(0)
-        w_cq(2, banks)
-        accs.append(base(0, 3))
-        w_cq(3, w_t(3))
+        accs.append(base_passes(0, 2))
+        banks = transpose_w(2)
+        scale_quantise_b(b_bf, 0)
+        finish_w(2, banks)
+        accs.append(base_passes(0, 3))
+        finish_w(3, transpose_w(3))
         for tt in range(4):
-            lora(0, tt, accs[tt])
-        banks = w_t(4)
-        fin(0, 0, accs[0])
-        fin(0, 1, accs[1])
-        w_cq(4, banks)
-        fin(0, 2, accs[2])
-        fin(0, 3, accs[3])
-        b_scale_quantise(1)
+            adapter_pass(0, tt, accs[tt])
+        banks = transpose_w(4)
+        add_bias_store(0, 0, accs[0])
+        add_bias_store(0, 1, accs[1])
+        finish_w(4, banks)
+        add_bias_store(0, 2, accs[2])
+        add_bias_store(0, 3, accs[3])
+        scale_quantise_b(b_bf, 1)
 
-        for m in range(2, 8):
-            g = m // 2
+        for step in range(2, W_UNITS):
+            g = step // 2
+            tiles = (2 * (step % 2), 2 * (step % 2) + 1)
             accs = []
-            for tt in (2 * (m % 2), 2 * (m % 2) + 1):
-                acc = base(g, tt)
-                lora(g, tt, acc)
+            for tt in tiles:
+                acc = base_passes(g, tt)
+                adapter_pass(g, tt, acc)
                 accs.append(acc)
-            banks = w_t(m + 3) if m + 3 < 8 else None
-            fin(g, 2 * (m % 2), accs[0])
-            fin(g, 2 * (m % 2) + 1, accs[1])
-            if m + 3 < 8:
-                w_cq(m + 3, banks)
+            banks = transpose_w(step + AHEAD) if step + AHEAD < W_UNITS else None
+            for tt, acc in zip(tiles, accs):
+                add_bias_store(g, tt, acc)
+            if step + AHEAD < W_UNITS:
+                finish_w(step + AHEAD, banks)

from contextlib import ExitStack

import concourse.mybir as mybir
from concourse.masks import make_identity

F32 = mybir.dt.float32
BF16 = mybir.dt.bfloat16
U32 = mybir.dt.uint32
U8 = mybir.dt.uint8
FP8X4 = mybir.dt.float8_e4m3fn_x4
ADD = mybir.AluOpType.add
MULT = mybir.AluOpType.mult

P = 128
TOKENS = 512
D_IN = 2048
D_OUT = 2048
ADAPTERS = 32
RANK = 16
K_LORA = ADAPTERS * RANK
SCALE = 2.0
PASSES = D_IN // 512
GROUP = 512
UNIT = 256
W_UNITS = D_OUT // UNIT
B_RUN = 16 * RANK
AHEAD = 3
FLOPS = 2 * TOKENS * D_IN * D_OUT + 2 * TOKENS * D_IN * K_LORA + 2 * TOKENS * K_LORA * D_OUT


def tile_replaced_compose_lora_pa_kernel(tc, x, lora_A, lora_B, W, bias, lora_weights, out):
    nc = tc.nc
    with ExitStack() as ctx:
        keep = ctx.enter_context(tc.tile_pool(name="keep", bufs=1))
        raw = ctx.enter_context(tc.tile_pool(name="raw", bufs=4))
        bpool = ctx.enter_context(tc.tile_pool(name="bpool", bufs=2))
        grp = ctx.enter_context(tc.tile_pool(name="grp", bufs=3))
        outp = ctx.enter_context(tc.tile_pool(name="outp", bufs=6))
        tps = ctx.enter_context(tc.psum_pool(name="tps", bufs=4))
        accp = ctx.enter_context(tc.psum_pool(name="accp", bufs=4))
        ctx.enter_context(tc.manual_schedule())

        x_rows = x.rearrange("b s d -> (b s) d").rearrange("(i p) d -> p i d", p=P)
        a_rows = lora_A.rearrange("n r d -> (n r) d").rearrange("(q t) d -> q t d", t=4)
        w_rows = W.rearrange("(i p) d -> p i d", p=P)
        b_rows = lora_B.rearrange("n (p l) r -> p n (l r)", l=16)
        out_rows = out.rearrange("b s o -> (b s) o")

        ident = keep.tile([P, P], F32, name="ident")
        make_identity(nc, ident[:])

        x_codes = keep.tile([P, PASSES, GROUP], U32, name="x_codes", align_bytes=64)
        x_scales = keep.tile([P, PASSES, GROUP], U8, name="x_scales", align_bytes=64)
        a_codes = keep.tile([P, PASSES, GROUP], U32, name="a_codes", align_bytes=64)
        a_scales = keep.tile([P, PASSES, GROUP], U8, name="a_scales", align_bytes=64)
        w_codes = keep.tile([P, D_OUT // GROUP, PASSES, GROUP], U32, name="w_codes", align_bytes=64)
        w_scales = keep.tile([P, D_OUT // GROUP, PASSES, GROUP], U8, name="w_scales", align_bytes=64)
        b_codes = keep.tile([P, D_OUT], U32, name="b_codes", align_bytes=64)
        b_scales = keep.tile([P, D_OUT], U8, name="b_scales", align_bytes=64)
        h_codes = keep.tile([P, TOKENS], U32, name="h_codes", align_bytes=64)
        h_scales = keep.tile([P, TOKENS], U8, name="h_scales", align_bytes=64)
        h_bf = keep.tile([P, TOKENS * 4], BF16, name="h_bf", align_bytes=64)
        bias_all = keep.tile([P, D_OUT], BF16, name="bias_all")
        lw_all = keep.tile([P, ADAPTERS], BF16, name="lw_all")
        picked = keep.tile([P, P], F32, name="picked")
        lw_own = keep.tile([P, 1], F32, name="lw_own")
        coef = keep.tile([P, 1], F32, name="coef")

        def load_group(rows, first, name):
            group = raw.tile([P, 4 * D_IN], BF16, tag="raw", name=name)
            for i in range(4):
                nc.sync.dma_start(out=group[:, i * D_IN:(i + 1) * D_IN], in_=rows[:, first + i, :])
            return group

        x_raw = load_group(x_rows, 0, "x_raw")
        nc.sync.dma_start(out=lw_all[:], in_=lora_weights.partition_broadcast(P))
        a_raw = load_group(a_rows, 0, "a_raw")
        w_raw = [load_group(w_rows, 0, "w_raw0")]
        b_raw = bpool.tile([P, ADAPTERS * B_RUN], BF16, tag="b", name="b_raw", align_bytes=64)
        for half in range(2):
            nc.sync.dma_start(
                out=b_raw[:, half * 4096:(half + 1) * 4096].rearrange("p (n k) -> p n k", k=B_RUN),
                in_=b_rows[:, half * 16:(half + 1) * 16, :],
            )
        w_raw.append(load_group(w_rows, 4, "w_raw1"))
        nc.sync.dma_start(out=bias_all[:], in_=bias.partition_broadcast(P))

        def transpose_unit(group, unit):
            words = group[:].bitcast(F32).rearrange("p (i w) -> p i w", i=4)
            banks = []
            for i in (2 * unit, 2 * unit + 1):
                for b in range(2):
                    bank = tps.tile([P, 512], F32, tag="tp", name="bank")
                    for u in range(2):
                        for c in range(2):
                            first = (2 * (2 * b + c) + u) * P
                            nc.tensor.transpose(
                                bank[:, (2 * u + c) * P:(2 * u + c + 1) * P], words[:, i, first:first + P], ident[:]
                            )
                    banks.append(bank)
            return banks

        def regroup_unit(banks):
            grouped = grp.tile([P, PASSES * UNIT * 4], BF16, tag="grp", name="grouped", align_bytes=64)
            words = grouped[:].bitcast(F32).rearrange("p (c r u) -> p c r u", c=PASSES, u=2)
            for i in range(2):
                for b in range(2):
                    nc.scalar.copy(
                        out=words[:, 2 * b:2 * b + 2, i * P:(i + 1) * P, :],
                        in_=banks[2 * i + b][:].rearrange("p (u c r) -> p c r u", u=2, c=2),
                    )
            return grouped

        def quantise_unit(grouped, unit, codes, scales):
            rows = slice(unit * UNIT, (unit + 1) * UNIT)
            for c in range(PASSES):
                nc.vector.quantize_mx(
                    out=codes[:, c, rows].bitcast(FP8X4),
                    scales=scales[:, c, rows],
                    in_=grouped[:, c * UNIT * 4:(c + 1) * UNIT * 4],
                )

        def transpose_w(k):
            return transpose_unit(w_raw[k // 2], k % 2)

        def finish_w(k, banks):
            quantise_unit(regroup_unit(banks), k % 2, w_codes[:, k // 2, :, :], w_scales[:, k // 2, :, :])

        h_banks = []

        def h_groups(tt, ts):
            tokens = slice(tt * P, (tt + 1) * P)
            for t in ts:
                for c in range(PASSES):
                    nc.tensor.matmul_mx(
                        out=h_banks[tt][:, t * P:(t + 1) * P],
                        lhsT=a_codes[:, c, t * P:(t + 1) * P].bitcast(FP8X4),
                        lhsT_scale=a_scales[:, c, t * P:(t + 1) * P],
                        rhs=x_codes[:, c, tokens].bitcast(FP8X4),
                        rhs_scale=x_scales[:, c, tokens],
                        start=(c == 0),
                        stop=(c == PASSES - 1),
                    )

        b_sorted = bpool.tile([P, ADAPTERS * B_RUN], BF16, tag="b", name="b_sorted", align_bytes=64)
        b_from = b_raw[:].bitcast(F32).rearrange("p (n l s u) -> p l u n s", n=ADAPTERS, l=16, s=4, u=2)
        b_words = b_sorted[:].bitcast(F32)
        b_to = b_words.rearrange("p (l u n s) -> p l u n s", l=16, u=2, n=ADAPTERS, s=4)

        def sort_b(half):
            adapters = slice(half * 16, (half + 1) * 16)
            for u in range(2):
                nc.vector.tensor_copy(out=b_to[:, :, u, adapters, :], in_=b_from[:, :, u, adapters, :])

        def scale_quantise_b(b_bf, half):
            part = b_bf[:, half * 4096:(half + 1) * 4096]
            nc.vector.tensor_scalar(out=part, in0=part, scalar1=coef[:, 0:1], scalar2=None, op0=MULT)
            nc.vector.quantize_mx(
                out=b_codes[:, half * 1024:(half + 1) * 1024].bitcast(FP8X4),
                scales=b_scales[:, half * 1024:(half + 1) * 1024],
                in_=part,
            )

        def base_passes(g, tt):
            acc = accp.tile([P, GROUP], F32, tag="acc", name="acc")
            tokens = slice(tt * P, (tt + 1) * P)
            for c in range(PASSES):
                nc.tensor.matmul_mx(
                    out=acc[:],
                    lhsT=x_codes[:, c, tokens].bitcast(FP8X4),
                    lhsT_scale=x_scales[:, c, tokens],
                    rhs=w_codes[:, g, c, :].bitcast(FP8X4),
                    rhs_scale=w_scales[:, g, c, :],
                    start=(c == 0),
                    stop=False,
                )
            return acc

        def adapter_pass(g, tt, acc):
            nc.tensor.matmul_mx(
                out=acc[:],
                lhsT=h_codes[:, tt * P:(tt + 1) * P].bitcast(FP8X4),
                lhsT_scale=h_scales[:, tt * P:(tt + 1) * P],
                rhs=b_codes[:, g * GROUP:(g + 1) * GROUP].bitcast(FP8X4),
                rhs_scale=b_scales[:, g * GROUP:(g + 1) * GROUP],
                start=False,
                stop=True,
            )

        def add_bias_store(g, tt, acc):
            result = outp.tile([P, GROUP], F32, tag="o", name="result")
            nc.vector.tensor_tensor(out=result[:], in0=acc[:], in1=bias_all[:, g * GROUP:(g + 1) * GROUP], op=ADD)
            nc.sync.dma_start(out=out_rows[tt * P:(tt + 1) * P, g * GROUP:(g + 1) * GROUP], in_=result[:])

        for group, codes, scales in ((x_raw, x_codes, x_scales), (a_raw, a_codes, a_scales)):
            for unit in range(2):
                quantise_unit(regroup_unit(transpose_unit(group, unit)), unit, codes, scales)
        w_raw.append(load_group(w_rows, 8, "w_raw2"))
        w_raw.append(load_group(w_rows, 12, "w_raw3"))

        nc.vector.tensor_tensor(
            out=picked[:].rearrange("p (n s) -> p n s", s=4),
            in0=ident[:].rearrange("p (n s) -> p n s", s=4),
            in1=lw_all[:].unsqueeze(2).to_broadcast([P, ADAPTERS, 4]),
            op=MULT,
        )
        nc.vector.tensor_reduce(out=lw_own[:], in_=picked[:], axis=mybir.AxisListType.X, op=ADD)
        nc.vector.tensor_scalar(out=coef[:], in0=lw_own[:], scalar1=SCALE, scalar2=None, op0=MULT)

        finish_w(0, transpose_w(0))
        for tt in range(4):
            h_bank = accp.tile([P, 512], F32, tag="acc", name="h_bank")
            h_banks.append(h_bank)
            h_groups(tt, (0, 1))
        grouped = regroup_unit(transpose_w(1))
        sort_b(0)
        quantise_unit(grouped, 1, w_codes[:, 0, :, :], w_scales[:, 0, :, :])
        for tt in range(4):
            h_groups(tt, (2, 3))
            nc.scalar.copy(
                out=h_bf[:, tt * 512:(tt + 1) * 512].rearrange("q (r t) -> q r t", t=4),
                in_=h_banks[tt][:].rearrange("q (t r) -> q r t", t=4),
            )
        sort_b(1)
        nc.vector.quantize_mx(out=h_codes[:].bitcast(FP8X4), scales=h_scales[:], in_=h_bf[:])

        accs = [base_passes(0, 0), base_passes(0, 1)]

        b_bf = bpool.tile([P, D_OUT * 4], BF16, tag="b", name="b_bf", align_bytes=64)
        b_out = b_bf[:].bitcast(F32).rearrange("q (p j a) -> q p j a", p=P, j=8, a=4)
        for j in range(8):
            bank = tps.tile([P, 512], F32, tag="tp", name="b_bank")
            for a in range(4):
                nc.tensor.transpose(bank[:, a * P:(a + 1) * P], b_words[:, (4 * j + a) * P:(4 * j + a + 1) * P], ident[:])
            if (j // 2) % 2 == 0:
                nc.scalar.copy(out=b_out[:, :, j, :], in_=bank[:].rearrange("q (a p) -> q p a", a=4))
            else:
                nc.vector.tensor_copy(out=b_out[:, :, j, :], in_=bank[:].rearrange("q (a p) -> q p a", a=4))

        accs.append(base_passes(0, 2))
        banks = transpose_w(2)
        scale_quantise_b(b_bf, 0)
        finish_w(2, banks)
        accs.append(base_passes(0, 3))
        finish_w(3, transpose_w(3))
        for tt in range(4):
            adapter_pass(0, tt, accs[tt])
        banks = transpose_w(4)
        add_bias_store(0, 0, accs[0])
        add_bias_store(0, 1, accs[1])
        finish_w(4, banks)
        add_bias_store(0, 2, accs[2])
        add_bias_store(0, 3, accs[3])
        scale_quantise_b(b_bf, 1)

        for step in range(2, W_UNITS):
            g = step // 2
            tiles = (2 * (step % 2), 2 * (step % 2) + 1)
            accs = []
            for tt in tiles:
                acc = base_passes(g, tt)
                adapter_pass(g, tt, acc)
                accs.append(acc)
            banks = transpose_w(step + AHEAD) if step + AHEAD < W_UNITS else None
            for tt, acc in zip(tiles, accs):
                add_bias_store(g, tt, acc)
            if step + AHEAD < W_UNITS:
                finish_w(step + AHEAD, banks)
